import numpy as np
import ml_dtypes

BF16 = ml_dtypes.bfloat16


def bf(x):
    return np.asarray(x, np.float32).astype(BF16)


def f32(x):
    return np.asarray(x, np.float32)


def f64(x):
    return np.asarray(x).astype(np.float64)


def striped(idx):
    return np.tile(idx.reshape(-1, 16).T, (8, 1))


S, D, H, N = 512, 128, 512, 256
EPS = 1e-5


def setup_inputs():
    return {"table": bf(np.random.standard_normal((S, D))), "w": bf(np.random.standard_normal((D, H)) / np.sqrt(D)), "gain": f32(1.0 + 0.1 * np.random.standard_normal((H, 1))), "bias": f32(0.1 * np.random.standard_normal((H, 1))), "offs": striped(np.random.permutation(np.tile(np.arange(S), 2))[:N])}


def reference(table, w, gain, bias, offs):
    idx = offs[:16].T.reshape(-1)
    y = f64(w).T @ f64(table)[idx].T
    mu = y.mean(axis=0, keepdims=True)
    var = np.square(y - mu).mean(axis=0, keepdims=True)
    return (y - mu) / np.sqrt(var + EPS) * f64(gain) + f64(bias)

@@ -1,0 +1,75 @@
+import concourse.mybir as mybir
+from concourse.masks import make_identity
+
+P = 128
+S, D, H, N = 512, 128, 512, 256
+SB = S // P
+HB = H // P
+EPS = 1e-5
+FLOPS = 2 * D * H * N
+
+BF16, F32, U16 = mybir.dt.bfloat16, mybir.dt.float32, mybir.dt.uint16
+ACT = mybir.ActivationFunctionType
+ALU = mybir.AluOpType
+
+
+def tile_lineattention_kernel(tc, table, w, gain, bias, offs, out):
+    nc = tc.nc
+    with tc.tile_pool(name="held", bufs=1) as held, tc.psum_pool(name="psum", bufs=1) as psum:
+        offsets = held.tile([P, N // 16], U16, name="offsets")
+        nc.sync.dma_start(offsets[:], offs)
+        table_rows = held.tile([P, SB, D], BF16, name="table_rows")
+        nc.sync.dma_start(table_rows[:], table.rearrange("(s p) k -> p s k", p=P))
+        w_rows = held.tile([D, H], BF16, name="w_rows")
+        nc.scalar.dma_start(w_rows[:], w)
+        gain_cols = held.tile([P, HB], F32, name="gain_cols")
+        nc.scalar.dma_start(gain_cols[:], gain.rearrange("(p b) one -> p (b one)", b=HB))
+        bias_cols = held.tile([P, HB], F32, name="bias_cols")
+        nc.scalar.dma_start(bias_cols[:], bias.rearrange("(p b) one -> p (b one)", b=HB))
+        out_blocks = out.rearrange("(p b) j -> p b j", b=HB)
+
+        identity = held.tile([P, P], BF16, name="identity")
+        make_identity(nc, identity[:])
+        averaging = held.tile([P, P], F32, name="averaging")
+        nc.vector.memset(averaging[:], 1.0 / H)
+        eps_col = held.tile([P, 1], F32, name="eps_col")
+        nc.vector.memset(eps_col[:], EPS)
+
+        flipped_ps = psum.tile([D, S], BF16, name="flipped_ps")
+        for s in range(SB):
+            nc.tensor.transpose(flipped_ps[:, s * P : (s + 1) * P], table_rows[:, s, :], identity[:])
+        table_cols = held.tile([D, S], BF16, name="table_cols")
+        nc.vector.tensor_copy(table_cols[:], flipped_ps[:])
+
+        w_blocks = held.tile([D, HB, P], BF16, name="w_blocks")
+        nc.vector.tensor_copy(w_blocks[:], w_rows[:].rearrange("k (p b) -> k b p", b=HB))
+
+        y = held.tile([P, HB, N], F32, name="y")
+        for b in range(HB):
+            y_ps = psum.tile([P, N], F32, name=f"y_ps{b}")
+            nc.tensor.matmul(y_ps[:], w_blocks[:, b, :], table_cols[:].indirect(offsets[:]), start=True, stop=True)
+            nc.scalar.activation(y[:, b, :], y_ps[:], ACT.Copy)
+
+        mean_ps = psum.tile([P, N], F32, name="mean_ps")
+        for b in range(HB):
+            nc.tensor.matmul(mean_ps[:], averaging[:], y[:, b, :], start=(b == 0), stop=(b == HB - 1))
+        centred = held.tile([P, HB, N], F32, name="centred")
+        squares = held.tile([P, HB, N], F32, name="squares")
+        var_ps = psum.tile([P, N], F32, name="var_ps")
+        for b in range(HB):
+            nc.vector.tensor_tensor(centred[:, b, :], y[:, b, :], mean_ps[:], ALU.subtract)
+            nc.scalar.activation(squares[:, b, :], centred[:, b, :], ACT.Square)
+            nc.tensor.matmul(var_ps[:], averaging[:], squares[:, b, :], start=(b == 0), stop=(b == HB - 1))
+        std = held.tile([P, N], F32, name="std")
+        nc.scalar.activation(std[:], var_ps[:], ACT.Sqrt, bias=eps_col[:], scale=1.0)
+        rstd = held.tile([P, N], F32, name="rstd")
+        nc.vector.reciprocal(rstd[:], std[:])
+
+        normed = held.tile([P, HB, N], F32, name="normed")
+        result = held.tile([P, HB, N], F32, name="result")
+        for b in range(HB):
+            nc.vector.tensor_tensor(normed[:, b, :], centred[:, b, :], rstd[:], ALU.mult)
+            nc.scalar.activation(
+                result[:, b, :], normed[:, b, :], ACT.Identity, bias=bias_cols[:, b : b + 1], scale=gain_cols[:, b : b + 1]
+            )
+            nc.sync.dma_start(out_blocks[:, b, :], result[:, b, :])

@@ -11,21 +11,22 @@ FLOPS = 2 * D * H * N
 BF16, F32, U16 = mybir.dt.bfloat16, mybir.dt.float32, mybir.dt.uint16
 ACT = mybir.ActivationFunctionType
 ALU = mybir.AluOpType
+AXIS = mybir.AxisListType
 
 
 def tile_lineattention_kernel(tc, table, w, gain, bias, offs, out):
     nc = tc.nc
     with tc.tile_pool(name="held", bufs=1) as held, tc.psum_pool(name="psum", bufs=1) as psum:
-        offsets = held.tile([P, N // 16], U16, name="offsets")
-        nc.sync.dma_start(offsets[:], offs)
         table_rows = held.tile([P, SB, D], BF16, name="table_rows")
         nc.sync.dma_start(table_rows[:], table.rearrange("(s p) k -> p s k", p=P))
         w_rows = held.tile([D, H], BF16, name="w_rows")
         nc.scalar.dma_start(w_rows[:], w)
+        offsets = held.tile([P, N // 16], U16, name="offsets")
+        nc.sync.dma_start(offsets[:], offs)
         gain_cols = held.tile([P, HB], F32, name="gain_cols")
-        nc.scalar.dma_start(gain_cols[:], gain.rearrange("(p b) one -> p (b one)", b=HB))
+        nc.sync.dma_start(gain_cols[:], gain.rearrange("(p b) one -> p (b one)", b=HB))
         bias_cols = held.tile([P, HB], F32, name="bias_cols")
-        nc.scalar.dma_start(bias_cols[:], bias.rearrange("(p b) one -> p (b one)", b=HB))
+        nc.sync.dma_start(bias_cols[:], bias.rearrange("(p b) one -> p (b one)", b=HB))
         out_blocks = out.rearrange("(p b) j -> p b j", b=HB)
 
         identity = held.tile([P, P], BF16, name="identity")
@@ -34,32 +35,39 @@ def tile_lineattention_kernel(tc, table, w, gain, bias, offs, out):
         nc.vector.memset(averaging[:], 1.0 / H)
         eps_col = held.tile([P, 1], F32, name="eps_col")
         nc.vector.memset(eps_col[:], EPS)
+        table_fetch = held.tile([P, 1], F32, name="table_fetch")
+        nc.scalar.activation(table_fetch[:], eps_col[:], ACT.Sqrt)
 
         flipped_ps = psum.tile([D, S], BF16, name="flipped_ps")
         for s in range(SB):
             nc.tensor.transpose(flipped_ps[:, s * P : (s + 1) * P], table_rows[:, s, :], identity[:])
         table_cols = held.tile([D, S], BF16, name="table_cols")
-        nc.vector.tensor_copy(table_cols[:], flipped_ps[:])
+        nc.scalar.copy(table_cols[:], flipped_ps[:])
 
-        w_blocks = held.tile([D, HB, P], BF16, name="w_blocks")
-        nc.vector.tensor_copy(w_blocks[:], w_rows[:].rearrange("k (p b) -> k b p", b=HB))
-
-        y = held.tile([P, HB, N], F32, name="y")
-        for b in range(HB):
-            y_ps = psum.tile([P, N], F32, name=f"y_ps{b}")
-            nc.tensor.matmul(y_ps[:], w_blocks[:, b, :], table_cols[:].indirect(offsets[:]), start=True, stop=True)
-            nc.scalar.activation(y[:, b, :], y_ps[:], ACT.Copy)
-
-        mean_ps = psum.tile([P, N], F32, name="mean_ps")
-        for b in range(HB):
-            nc.tensor.matmul(mean_ps[:], averaging[:], y[:, b, :], start=(b == 0), stop=(b == HB - 1))
-        centred = held.tile([P, HB, N], F32, name="centred")
+        w_sum = held.tile([D, 1], F32, name="w_sum")
+        nc.vector.reduce_sum(w_sum[:], w_rows[:], AXIS.X)
+        neg_mean = held.tile([D, 1], F32, name="neg_mean")
+        nc.vector.tensor_scalar(neg_mean[:], w_sum[:], -1.0 / H, None, ALU.mult)
+        w_by_block = w_rows[:].rearrange("k (p b) -> k b p", b=HB)
+        w_hi = held.tile([D, HB, P], BF16, name="w_hi")
+        w_lo = held.tile([D, HB, P], BF16, name="w_lo")
+        centred_ps = [psum.tile([P, N], F32, name=f"centred_ps{b}") for b in range(HB)]
         squares = held.tile([P, HB, N], F32, name="squares")
-        var_ps = psum.tile([P, N], F32, name="var_ps")
         for b in range(HB):
-            nc.vector.tensor_tensor(centred[:, b, :], y[:, b, :], mean_ps[:], ALU.subtract)
-            nc.scalar.activation(squares[:, b, :], centred[:, b, :], ACT.Square)
-            nc.tensor.matmul(var_ps[:], averaging[:], squares[:, b, :], start=(b == 0), stop=(b == HB - 1))
+            nc.vector.tensor_scalar(w_hi[:, b, :], w_by_block[:, b, :], neg_mean[:], None, ALU.add)
+            nc.vector.scalar_tensor_tensor(
+                w_lo[:, b, :], w_by_block[:, b, :], neg_mean[:], w_hi[:, b, :], ALU.add, ALU.subtract
+            )
+            nc.tensor.matmul(centred_ps[b][:], w_hi[:, b, :], table_cols[:].indirect(offsets[:]), start=True, stop=False)
+            nc.tensor.matmul(centred_ps[b][:], w_lo[:, b, :], table_cols[:].indirect(offsets[:]), start=False, stop=True)
+            nc.scalar.activation(squares[:, b, :], centred_ps[b][:], ACT.Square)
+
+        square_sums = held.tile([P, HB - 1, N], F32, name="square_sums")
+        nc.vector.tensor_tensor(square_sums[:, 0, :], squares[:, 0, :], squares[:, 1, :], ALU.add)
+        for b in range(2, HB):
+            nc.vector.tensor_tensor(square_sums[:, b - 1, :], square_sums[:, b - 2, :], squares[:, b, :], ALU.add)
+        var_ps = psum.tile([P, N], F32, name="var_ps")
+        nc.tensor.matmul(var_ps[:], averaging[:], square_sums[:, HB - 2, :], start=True, stop=True)
         std = held.tile([P, N], F32, name="std")
         nc.scalar.activation(std[:], var_ps[:], ACT.Sqrt, bias=eps_col[:], scale=1.0)
         rstd = held.tile([P, N], F32, name="rstd")
@@ -68,7 +76,7 @@ def tile_lineattention_kernel(tc, table, w, gain, bias, offs, out):
         normed = held.tile([P, HB, N], F32, name="normed")
         result = held.tile([P, HB, N], F32, name="result")
         for b in range(HB):
-            nc.vector.tensor_tensor(normed[:, b, :], centred[:, b, :], rstd[:], ALU.mult)
+            nc.vector.tensor_tensor(normed[:, b, :], centred_ps[b][:], rstd[:], ALU.mult)
             nc.scalar.activation(
                 result[:, b, :], normed[:, b, :], ACT.Identity, bias=bias_cols[:, b : b + 1], scale=gain_cols[:, b : b + 1]
             )

@@ -7,6 +7,8 @@ SB = S // P
 HB = H // P
 EPS = 1e-5
 FLOPS = 2 * D * H * N
+WARM_BEFORE = 4
+WARM_BETWEEN = 2
 
 BF16, F32, U16 = mybir.dt.bfloat16, mybir.dt.float32, mybir.dt.uint16
 ACT = mybir.ActivationFunctionType
@@ -35,6 +37,11 @@ def tile_lineattention_kernel(tc, table, w, gain, bias, offs, out):
         nc.vector.memset(averaging[:], 1.0 / H)
         eps_col = held.tile([P, 1], F32, name="eps_col")
         nc.vector.memset(eps_col[:], EPS)
+        zeros = held.tile([P, S], BF16, name="zeros")
+        nc.vector.memset(zeros[:], 0.0)
+        unread_ps = psum.tile([P, S], F32, name="unread_ps")
+        for i in range(WARM_BEFORE):
+            nc.tensor.matmul(unread_ps[:], zeros[:, 0:P], zeros[:], start=True, stop=True)
         table_fetch = held.tile([P, 1], F32, name="table_fetch")
         nc.scalar.activation(table_fetch[:], eps_col[:], ACT.Sqrt)
 
@@ -43,6 +50,8 @@ def tile_lineattention_kernel(tc, table, w, gain, bias, offs, out):
             nc.tensor.transpose(flipped_ps[:, s * P : (s + 1) * P], table_rows[:, s, :], identity[:])
         table_cols = held.tile([D, S], BF16, name="table_cols")
         nc.scalar.copy(table_cols[:], flipped_ps[:])
+        for i in range(WARM_BETWEEN):
+            nc.tensor.matmul(unread_ps[:], identity[:], table_rows[:].rearrange("p s k -> p (s k)"), start=True, stop=True)
 
         w_sum = held.tile([D, 1], F32, name="w_sum")
         nc.vector.reduce_sum(w_sum[:], w_rows[:], AXIS.X)

@@ -7,8 +7,6 @@ SB = S // P
 HB = H // P
 EPS = 1e-5
 FLOPS = 2 * D * H * N
-WARM_BEFORE = 4
-WARM_BETWEEN = 2
 
 BF16, F32, U16 = mybir.dt.bfloat16, mybir.dt.float32, mybir.dt.uint16
 ACT = mybir.ActivationFunctionType
@@ -37,21 +35,14 @@ def tile_lineattention_kernel(tc, table, w, gain, bias, offs, out):
         nc.vector.memset(averaging[:], 1.0 / H)
         eps_col = held.tile([P, 1], F32, name="eps_col")
         nc.vector.memset(eps_col[:], EPS)
-        zeros = held.tile([P, S], BF16, name="zeros")
-        nc.vector.memset(zeros[:], 0.0)
-        unread_ps = psum.tile([P, S], F32, name="unread_ps")
-        for i in range(WARM_BEFORE):
-            nc.tensor.matmul(unread_ps[:], zeros[:, 0:P], zeros[:], start=True, stop=True)
         table_fetch = held.tile([P, 1], F32, name="table_fetch")
-        nc.scalar.activation(table_fetch[:], eps_col[:], ACT.Sqrt)
+        nc.scalar.activation(table_fetch[:], eps_col[:], ACT.Abs_reciprocal_sqrt)
 
         flipped_ps = psum.tile([D, S], BF16, name="flipped_ps")
         for s in range(SB):
             nc.tensor.transpose(flipped_ps[:, s * P : (s + 1) * P], table_rows[:, s, :], identity[:])
         table_cols = held.tile([D, S], BF16, name="table_cols")
         nc.scalar.copy(table_cols[:], flipped_ps[:])
-        for i in range(WARM_BETWEEN):
-            nc.tensor.matmul(unread_ps[:], identity[:], table_rows[:].rearrange("p s k -> p (s k)"), start=True, stop=True)
 
         w_sum = held.tile([D, 1], F32, name="w_sum")
         nc.vector.reduce_sum(w_sum[:], w_rows[:], AXIS.X)
@@ -77,10 +68,8 @@ def tile_lineattention_kernel(tc, table, w, gain, bias, offs, out):
             nc.vector.tensor_tensor(square_sums[:, b - 1, :], square_sums[:, b - 2, :], squares[:, b, :], ALU.add)
         var_ps = psum.tile([P, N], F32, name="var_ps")
         nc.tensor.matmul(var_ps[:], averaging[:], square_sums[:, HB - 2, :], start=True, stop=True)
-        std = held.tile([P, N], F32, name="std")
-        nc.scalar.activation(std[:], var_ps[:], ACT.Sqrt, bias=eps_col[:], scale=1.0)
         rstd = held.tile([P, N], F32, name="rstd")
-        nc.vector.reciprocal(rstd[:], std[:])
+        nc.scalar.activation(rstd[:], var_ps[:], ACT.Abs_reciprocal_sqrt, bias=eps_col[:], scale=1.0)
 
         normed = held.tile([P, HB, N], F32, name="normed")
         result = held.tile([P, HB, N], F32, name="result")

@@ -18,7 +18,9 @@ def tile_lineattention_kernel(tc, table, w, gain, bias, offs, out):
     nc = tc.nc
     with tc.tile_pool(name="held", bufs=1) as held, tc.psum_pool(name="psum", bufs=1) as psum:
         table_rows = held.tile([P, SB, D], BF16, name="table_rows")
-        nc.sync.dma_start(table_rows[:], table.rearrange("(s p) k -> p s k", p=P))
+        table_blocks = table.rearrange("(s p) k -> p s k", p=P)
+        for s in range(SB):
+            nc.sync.dma_start(table_rows[:, s, :], table_blocks[:, s, :])
         w_rows = held.tile([D, H], BF16, name="w_rows")
         nc.scalar.dma_start(w_rows[:], w)
         offsets = held.tile([P, N // 16], U16, name="offsets")
@@ -38,11 +40,12 @@ def tile_lineattention_kernel(tc, table, w, gain, bias, offs, out):
         table_fetch = held.tile([P, 1], F32, name="table_fetch")
         nc.scalar.activation(table_fetch[:], eps_col[:], ACT.Abs_reciprocal_sqrt)
 
-        flipped_ps = psum.tile([D, S], BF16, name="flipped_ps")
-        for s in range(SB):
-            nc.tensor.transpose(flipped_ps[:, s * P : (s + 1) * P], table_rows[:, s, :], identity[:])
         table_cols = held.tile([D, S], BF16, name="table_cols")
-        nc.scalar.copy(table_cols[:], flipped_ps[:])
+        for half in range(2):
+            flipped_ps = psum.tile([D, 2 * P], BF16, name=f"flipped_ps{half}")
+            for i in range(2):
+                nc.tensor.transpose(flipped_ps[:, i * P : (i + 1) * P], table_rows[:, 2 * half + i, :], identity[:])
+            nc.scalar.copy(table_cols[:, half * 2 * P : (half + 1) * 2 * P], flipped_ps[:])
 
         w_sum = held.tile([D, 1], F32, name="w_sum")
         nc.vector.reduce_sum(w_sum[:], w_rows[:], AXIS.X)
@@ -62,12 +65,14 @@ def tile_lineattention_kernel(tc, table, w, gain, bias, offs, out):
             nc.tensor.matmul(centred_ps[b][:], w_lo[:, b, :], table_cols[:].indirect(offsets[:]), start=False, stop=True)
             nc.scalar.activation(squares[:, b, :], centred_ps[b][:], ACT.Square)
 
-        square_sums = held.tile([P, HB - 1, N], F32, name="square_sums")
-        nc.vector.tensor_tensor(square_sums[:, 0, :], squares[:, 0, :], squares[:, 1, :], ALU.add)
-        for b in range(2, HB):
-            nc.vector.tensor_tensor(square_sums[:, b - 1, :], square_sums[:, b - 2, :], squares[:, b, :], ALU.add)
+        last = HB - 1
+        square_sums = held.tile([P, N], F32, name="square_sums")
+        nc.vector.tensor_tensor(square_sums[:], squares[:, 0, :], squares[:, 1, :], ALU.add)
+        for b in range(2, last):
+            nc.vector.tensor_tensor(square_sums[:], square_sums[:], squares[:, b, :], ALU.add)
         var_ps = psum.tile([P, N], F32, name="var_ps")
-        nc.tensor.matmul(var_ps[:], averaging[:], square_sums[:, HB - 2, :], start=True, stop=True)
+        nc.tensor.matmul(var_ps[:], averaging[:], squares[:, last, :], start=True, stop=False)
+        nc.tensor.matmul(var_ps[:], averaging[:], square_sums[:], start=False, stop=True)
         rstd = held.tile([P, N], F32, name="rstd")
         nc.scalar.activation(rstd[:], var_ps[:], ACT.Abs_reciprocal_sqrt, bias=eps_col[:], scale=1.0)
 

@@ -5,6 +5,8 @@ P = 128
 S, D, H, N = 512, 128, 512, 256
 SB = S // P
 HB = H // P
+NH = 2
+NW = N // NH
 EPS = 1e-5
 FLOPS = 2 * D * H * N
 
@@ -70,17 +72,22 @@ def tile_lineattention_kernel(tc, table, w, gain, bias, offs, out):
         nc.vector.tensor_tensor(square_sums[:], squares[:, 0, :], squares[:, 1, :], ALU.add)
         for b in range(2, last):
             nc.vector.tensor_tensor(square_sums[:], square_sums[:], squares[:, b, :], ALU.add)
-        var_ps = psum.tile([P, N], F32, name="var_ps")
-        nc.tensor.matmul(var_ps[:], averaging[:], squares[:, last, :], start=True, stop=False)
-        nc.tensor.matmul(var_ps[:], averaging[:], square_sums[:], start=False, stop=True)
         rstd = held.tile([P, N], F32, name="rstd")
-        nc.scalar.activation(rstd[:], var_ps[:], ACT.Abs_reciprocal_sqrt, bias=eps_col[:], scale=1.0)
+        for h in range(NH):
+            cols = slice(h * NW, (h + 1) * NW)
+            var_ps = psum.tile([P, NW], F32, name=f"var_ps{h}")
+            nc.tensor.matmul(var_ps[:], averaging[:], squares[:, last, cols], start=True, stop=False)
+            nc.tensor.matmul(var_ps[:], averaging[:], square_sums[:, cols], start=False, stop=True)
+            nc.scalar.activation(rstd[:, cols], var_ps[:], ACT.Abs_reciprocal_sqrt, bias=eps_col[:], scale=1.0)
 
         normed = held.tile([P, HB, N], F32, name="normed")
         result = held.tile([P, HB, N], F32, name="result")
-        for b in range(HB):
-            nc.vector.tensor_tensor(normed[:, b, :], centred_ps[b][:], rstd[:], ALU.mult)
-            nc.scalar.activation(
-                result[:, b, :], normed[:, b, :], ACT.Identity, bias=bias_cols[:, b : b + 1], scale=gain_cols[:, b : b + 1]
-            )
-            nc.sync.dma_start(out_blocks[:, b, :], result[:, b, :])
+        for h in range(NH):
+            cols = slice(h * NW, (h + 1) * NW)
+            for b in range(HB):
+                nc.vector.tensor_tensor(normed[:, b, cols], centred_ps[b][:, cols], rstd[:, cols], ALU.mult)
+                nc.scalar.activation(
+                    result[:, b, cols], normed[:, b, cols], ACT.Identity, bias=bias_cols[:, b : b + 1], scale=gain_cols[:, b : b + 1]
+                )
+                if b % 2 == 1:
+                    nc.sync.dma_start(out_blocks[:, b - 1 : b + 1, cols], result[:, b - 1 : b + 1, cols])

@@ -65,19 +65,19 @@ def tile_lineattention_kernel(tc, table, w, gain, bias, offs, out):
             )
             nc.tensor.matmul(centred_ps[b][:], w_hi[:, b, :], table_cols[:].indirect(offsets[:]), start=True, stop=False)
             nc.tensor.matmul(centred_ps[b][:], w_lo[:, b, :], table_cols[:].indirect(offsets[:]), start=False, stop=True)
-            nc.scalar.activation(squares[:, b, :], centred_ps[b][:], ACT.Square)
+            for h in range(NH):
+                cols = slice(h * NW, (h + 1) * NW)
+                nc.scalar.activation(squares[:, b, cols], centred_ps[b][:, cols], ACT.Square)
 
-        last = HB - 1
-        square_sums = held.tile([P, N], F32, name="square_sums")
-        nc.vector.tensor_tensor(square_sums[:], squares[:, 0, :], squares[:, 1, :], ALU.add)
-        for b in range(2, last):
-            nc.vector.tensor_tensor(square_sums[:], square_sums[:], squares[:, b, :], ALU.add)
+        first_two = held.tile([P, N], F32, name="first_two")
+        nc.vector.tensor_tensor(first_two[:], squares[:, 0, :], squares[:, 1, :], ALU.add)
+        terms = [squares[:, 2, :], first_two[:], squares[:, 3, :]]
         rstd = held.tile([P, N], F32, name="rstd")
         for h in range(NH):
             cols = slice(h * NW, (h + 1) * NW)
             var_ps = psum.tile([P, NW], F32, name=f"var_ps{h}")
-            nc.tensor.matmul(var_ps[:], averaging[:], squares[:, last, cols], start=True, stop=False)
-            nc.tensor.matmul(var_ps[:], averaging[:], square_sums[:, cols], start=False, stop=True)
+            for i, term in enumerate(terms):
+                nc.tensor.matmul(var_ps[:], averaging[:], term[:, cols], start=(i == 0), stop=(i == len(terms) - 1))
             nc.scalar.activation(rstd[:, cols], var_ps[:], ACT.Abs_reciprocal_sqrt, bias=eps_col[:], scale=1.0)
 
         normed = held.tile([P, HB, N], F32, name="normed")

@@ -19,12 +19,12 @@ AXIS = mybir.AxisListType
 def tile_lineattention_kernel(tc, table, w, gain, bias, offs, out):
     nc = tc.nc
     with tc.tile_pool(name="held", bufs=1) as held, tc.psum_pool(name="psum", bufs=1) as psum:
+        w_rows = held.tile([D, H], BF16, name="w_rows")
+        nc.sync.dma_start(w_rows[:], w)
         table_rows = held.tile([P, SB, D], BF16, name="table_rows")
         table_blocks = table.rearrange("(s p) k -> p s k", p=P)
         for s in range(SB):
             nc.sync.dma_start(table_rows[:, s, :], table_blocks[:, s, :])
-        w_rows = held.tile([D, H], BF16, name="w_rows")
-        nc.scalar.dma_start(w_rows[:], w)
         offsets = held.tile([P, N // 16], U16, name="offsets")
         nc.sync.dma_start(offsets[:], offs)
         gain_cols = held.tile([P, HB], F32, name="gain_cols")
@@ -43,41 +43,62 @@ def tile_lineattention_kernel(tc, table, w, gain, bias, offs, out):
         nc.scalar.activation(table_fetch[:], eps_col[:], ACT.Abs_reciprocal_sqrt)
 
         table_cols = held.tile([D, S], BF16, name="table_cols")
-        for half in range(2):
-            flipped_ps = psum.tile([D, 2 * P], BF16, name=f"flipped_ps{half}")
-            for i in range(2):
-                nc.tensor.transpose(flipped_ps[:, i * P : (i + 1) * P], table_rows[:, 2 * half + i, :], identity[:])
-            nc.scalar.copy(table_cols[:, half * 2 * P : (half + 1) * 2 * P], flipped_ps[:])
+        for s in range(SB):
+            flipped_ps = psum.tile([D, P], BF16, name=f"flipped_ps{s}", tag=f"bank{s}")
+            nc.tensor.transpose(flipped_ps[:], table_rows[:, s, :], identity[:])
+            nc.scalar.copy(table_cols[:, s * P : (s + 1) * P], flipped_ps[:])
 
-        w_sum = held.tile([D, 1], F32, name="w_sum")
-        nc.vector.reduce_sum(w_sum[:], w_rows[:], AXIS.X)
-        neg_mean = held.tile([D, 1], F32, name="neg_mean")
-        nc.vector.tensor_scalar(neg_mean[:], w_sum[:], -1.0 / H, None, ALU.mult)
+        HH = H // 2
+        scaled = held.tile([D, H], F32, name="scaled")
+        neg_mean_a = held.tile([D, 1], F32, name="neg_mean_a")
+        neg_mean_b = held.tile([D, 1], F32, name="neg_mean_b")
+        nc.vector.tensor_scalar(scaled[:, :HH], w_rows[:, :HH], -1.0 / H, None, ALU.mult, ALU.add, accum_out=neg_mean_a[:])
+        nc.scalar.activation(scaled[:, HH:], w_rows[:, HH:], ACT.Copy, scale=-1.0 / H, accum_out=neg_mean_b[:])
         w_by_block = w_rows[:].rearrange("k (p b) -> k b p", b=HB)
         w_hi = held.tile([D, HB, P], BF16, name="w_hi")
         w_lo = held.tile([D, HB, P], BF16, name="w_lo")
-        centred_ps = [psum.tile([P, N], F32, name=f"centred_ps{b}") for b in range(HB)]
-        squares = held.tile([P, HB, N], F32, name="squares")
         for b in range(HB):
-            nc.vector.tensor_scalar(w_hi[:, b, :], w_by_block[:, b, :], neg_mean[:], None, ALU.add)
+            nc.vector.tensor_scalar(w_hi[:, b, :], w_by_block[:, b, :], neg_mean_a[:], neg_mean_b[:], ALU.add, ALU.add)
+        neg_mean = held.tile([D, 1], F32, name="neg_mean")
+        nc.vector.tensor_tensor(neg_mean[:], neg_mean_a[:], neg_mean_b[:], ALU.add)
+        for b in range(HB):
             nc.vector.scalar_tensor_tensor(
                 w_lo[:, b, :], w_by_block[:, b, :], neg_mean[:], w_hi[:, b, :], ALU.add, ALU.subtract
             )
-            nc.tensor.matmul(centred_ps[b][:], w_hi[:, b, :], table_cols[:].indirect(offsets[:]), start=True, stop=False)
-            nc.tensor.matmul(centred_ps[b][:], w_lo[:, b, :], table_cols[:].indirect(offsets[:]), start=False, stop=True)
-            for h in range(NH):
-                cols = slice(h * NW, (h + 1) * NW)
-                nc.scalar.activation(squares[:, b, cols], centred_ps[b][:, cols], ACT.Square)
+
+        centred_ps = [psum.tile([P, N], F32, name=f"centred_ps{b}", tag=f"bank{b}") for b in range(HB)]
+        squares = held.tile([P, HB, N], F32, name="squares")
+        for h in range(NH):
+            cols = slice(h * NW, (h + 1) * NW)
+            piece = offsets[:, h * (NW // 16) : (h + 1) * (NW // 16)]
+            if h == 0:
+                for b in range(HB):
+                    nc.tensor.matmul(centred_ps[b][:, cols], w_hi[:, b, :], table_cols[:].indirect(piece), start=True, stop=False)
+                for b in range(HB):
+                    nc.tensor.matmul(centred_ps[b][:, cols], w_lo[:, b, :], table_cols[:].indirect(piece), start=False, stop=True)
+                    nc.scalar.activation(squares[:, b, cols], centred_ps[b][:, cols], ACT.Square)
+            else:
+                for b in range(HB):
+                    nc.tensor.matmul(centred_ps[b][:, cols], w_hi[:, b, :], table_cols[:].indirect(piece), start=True, stop=False)
+                    nc.tensor.matmul(centred_ps[b][:, cols], w_lo[:, b, :], table_cols[:].indirect(piece), start=False, stop=True)
+                    nc.scalar.activation(squares[:, b, cols], centred_ps[b][:, cols], ACT.Square)
 
         first_two = held.tile([P, N], F32, name="first_two")
-        nc.vector.tensor_tensor(first_two[:], squares[:, 0, :], squares[:, 1, :], ALU.add)
-        terms = [squares[:, 2, :], first_two[:], squares[:, 3, :]]
+        last_two = held.tile([P, NW], F32, name="last_two")
+        all_four = held.tile([P, NW], F32, name="all_four")
+        first = slice(0, NW)
+        second = slice(NW, N)
+        nc.vector.tensor_tensor(first_two[:, first], squares[:, 0, first], squares[:, 1, first], ALU.add)
+        nc.vector.tensor_tensor(last_two[:], squares[:, 2, first], squares[:, 3, first], ALU.add)
+        nc.vector.tensor_tensor(all_four[:], first_two[:, first], last_two[:], ALU.add)
+        nc.vector.tensor_tensor(first_two[:, second], squares[:, 0, second], squares[:, 1, second], ALU.add)
+        terms = [[all_four[:]], [first_two[:, second], squares[:, 2, second], squares[:, 3, second]]]
         rstd = held.tile([P, N], F32, name="rstd")
         for h in range(NH):
             cols = slice(h * NW, (h + 1) * NW)
             var_ps = psum.tile([P, NW], F32, name=f"var_ps{h}")
-            for i, term in enumerate(terms):
-                nc.tensor.matmul(var_ps[:], averaging[:], term[:, cols], start=(i == 0), stop=(i == len(terms) - 1))
+            for i, term in enumerate(terms[h]):
+                nc.tensor.matmul(var_ps[:], averaging[:], term, start=(i == 0), stop=(i == len(terms[h]) - 1))
             nc.scalar.activation(rstd[:, cols], var_ps[:], ACT.Abs_reciprocal_sqrt, bias=eps_col[:], scale=1.0)
 
         normed = held.tile([P, HB, N], F32, name="normed")

@@ -57,11 +57,11 @@ def tile_lineattention_kernel(tc, table, w, gain, bias, offs, out):
         w_by_block = w_rows[:].rearrange("k (p b) -> k b p", b=HB)
         w_hi = held.tile([D, HB, P], BF16, name="w_hi")
         w_lo = held.tile([D, HB, P], BF16, name="w_lo")
+        neg_mean = held.tile([D, 1], F32, name="neg_mean")
         for b in range(HB):
             nc.vector.tensor_scalar(w_hi[:, b, :], w_by_block[:, b, :], neg_mean_a[:], neg_mean_b[:], ALU.add, ALU.add)
-        neg_mean = held.tile([D, 1], F32, name="neg_mean")
-        nc.vector.tensor_tensor(neg_mean[:], neg_mean_a[:], neg_mean_b[:], ALU.add)
-        for b in range(HB):
+            if b == 0:
+                nc.vector.tensor_tensor(neg_mean[:], neg_mean_a[:], neg_mean_b[:], ALU.add)
             nc.vector.scalar_tensor_tensor(
                 w_lo[:, b, :], w_by_block[:, b, :], neg_mean[:], w_hi[:, b, :], ALU.add, ALU.subtract
             )
@@ -71,28 +71,20 @@ def tile_lineattention_kernel(tc, table, w, gain, bias, offs, out):
         for h in range(NH):
             cols = slice(h * NW, (h + 1) * NW)
             piece = offsets[:, h * (NW // 16) : (h + 1) * (NW // 16)]
-            if h == 0:
-                for b in range(HB):
-                    nc.tensor.matmul(centred_ps[b][:, cols], w_hi[:, b, :], table_cols[:].indirect(piece), start=True, stop=False)
-                for b in range(HB):
-                    nc.tensor.matmul(centred_ps[b][:, cols], w_lo[:, b, :], table_cols[:].indirect(piece), start=False, stop=True)
-                    nc.scalar.activation(squares[:, b, cols], centred_ps[b][:, cols], ACT.Square)
-            else:
-                for b in range(HB):
-                    nc.tensor.matmul(centred_ps[b][:, cols], w_hi[:, b, :], table_cols[:].indirect(piece), start=True, stop=False)
-                    nc.tensor.matmul(centred_ps[b][:, cols], w_lo[:, b, :], table_cols[:].indirect(piece), start=False, stop=True)
-                    nc.scalar.activation(squares[:, b, cols], centred_ps[b][:, cols], ACT.Square)
+            for b in range(HB):
+                nc.tensor.matmul(centred_ps[b][:, cols], w_hi[:, b, :], table_cols[:].indirect(piece), start=True, stop=False)
+                nc.tensor.matmul(centred_ps[b][:, cols], w_lo[:, b, :], table_cols[:].indirect(piece), start=False, stop=True)
+                nc.scalar.activation(squares[:, b, cols], centred_ps[b][:, cols], ACT.Square)
 
-        first_two = held.tile([P, N], F32, name="first_two")
-        last_two = held.tile([P, NW], F32, name="last_two")
-        all_four = held.tile([P, NW], F32, name="all_four")
         first = slice(0, NW)
         second = slice(NW, N)
-        nc.vector.tensor_tensor(first_two[:, first], squares[:, 0, first], squares[:, 1, first], ALU.add)
-        nc.vector.tensor_tensor(last_two[:], squares[:, 2, first], squares[:, 3, first], ALU.add)
-        nc.vector.tensor_tensor(all_four[:], first_two[:, first], last_two[:], ALU.add)
-        nc.vector.tensor_tensor(first_two[:, second], squares[:, 0, second], squares[:, 1, second], ALU.add)
-        terms = [[all_four[:]], [first_two[:, second], squares[:, 2, second], squares[:, 3, second]]]
+        sum_a = held.tile([P, NW], F32, name="sum_a")
+        sum_b = held.tile([P, NW], F32, name="sum_b")
+        nc.vector.tensor_tensor(sum_a[:], squares[:, 0, first], squares[:, 1, first], ALU.add)
+        nc.vector.tensor_tensor(sum_b[:], sum_a[:], squares[:, 2, first], ALU.add)
+        nc.vector.tensor_tensor(sum_a[:], sum_b[:], squares[:, 3, first], ALU.add)
+        nc.vector.tensor_tensor(sum_b[:], squares[:, 0, second], squares[:, 1, second], ALU.add)
+        terms = [[sum_a[:]], [sum_b[:], squares[:, 2, second], squares[:, 3, second]]]
         rstd = held.tile([P, N], F32, name="rstd")
         for h in range(NH):
             cols = slice(h * NW, (h + 1) * NW)
@@ -107,8 +99,12 @@ def tile_lineattention_kernel(tc, table, w, gain, bias, offs, out):
             cols = slice(h * NW, (h + 1) * NW)
             for b in range(HB):
                 nc.vector.tensor_tensor(normed[:, b, cols], centred_ps[b][:, cols], rstd[:, cols], ALU.mult)
-                nc.scalar.activation(
-                    result[:, b, cols], normed[:, b, cols], ACT.Identity, bias=bias_cols[:, b : b + 1], scale=gain_cols[:, b : b + 1]
-                )
-                if b % 2 == 1:
-                    nc.sync.dma_start(out_blocks[:, b - 1 : b + 1, cols], result[:, b - 1 : b + 1, cols])
+                if h == 0 or b >= HB // 2:
+                    nc.vector.tensor_scalar(
+                        result[:, b, cols], normed[:, b, cols], gain_cols[:, b : b + 1], bias_cols[:, b : b + 1], ALU.mult, ALU.add
+                    )
+                else:
+                    nc.scalar.activation(
+                        result[:, b, cols], normed[:, b, cols], ACT.Identity, bias=bias_cols[:, b : b + 1], scale=gain_cols[:, b : b + 1]
+                    )
+                nc.sync.dma_start(out_blocks[:, b, cols], result[:, b, cols])

@@ -99,12 +99,7 @@ def tile_lineattention_kernel(tc, table, w, gain, bias, offs, out):
             cols = slice(h * NW, (h + 1) * NW)
             for b in range(HB):
                 nc.vector.tensor_tensor(normed[:, b, cols], centred_ps[b][:, cols], rstd[:, cols], ALU.mult)
-                if h == 0 or b >= HB // 2:
-                    nc.vector.tensor_scalar(
-                        result[:, b, cols], normed[:, b, cols], gain_cols[:, b : b + 1], bias_cols[:, b : b + 1], ALU.mult, ALU.add
-                    )
-                else:
-                    nc.scalar.activation(
-                        result[:, b, cols], normed[:, b, cols], ACT.Identity, bias=bias_cols[:, b : b + 1], scale=gain_cols[:, b : b + 1]
-                    )
+                nc.vector.tensor_scalar(
+                    result[:, b, cols], normed[:, b, cols], gain_cols[:, b : b + 1], bias_cols[:, b : b + 1], ALU.mult, ALU.add
+                )
                 nc.sync.dma_start(out_blocks[:, b, cols], result[:, b, cols])

@@ -19,11 +19,12 @@ AXIS = mybir.AxisListType
 def tile_lineattention_kernel(tc, table, w, gain, bias, offs, out):
     nc = tc.nc
     with tc.tile_pool(name="held", bufs=1) as held, tc.psum_pool(name="psum", bufs=1) as psum:
-        w_rows = held.tile([D, H], BF16, name="w_rows")
-        nc.sync.dma_start(w_rows[:], w)
         table_rows = held.tile([P, SB, D], BF16, name="table_rows")
         table_blocks = table.rearrange("(s p) k -> p s k", p=P)
-        for s in range(SB):
+        w_rows = held.tile([D, H], BF16, name="w_rows")
+        nc.sync.dma_start(table_rows[:, 0, :], table_blocks[:, 0, :])
+        nc.sync.dma_start(w_rows[:], w)
+        for s in range(1, SB):
             nc.sync.dma_start(table_rows[:, s, :], table_blocks[:, s, :])
         offsets = held.tile([P, N // 16], U16, name="offsets")
         nc.sync.dma_start(offsets[:], offs)
@@ -48,20 +49,14 @@ def tile_lineattention_kernel(tc, table, w, gain, bias, offs, out):
             nc.tensor.transpose(flipped_ps[:], table_rows[:, s, :], identity[:])
             nc.scalar.copy(table_cols[:, s * P : (s + 1) * P], flipped_ps[:])
 
-        HH = H // 2
-        scaled = held.tile([D, H], F32, name="scaled")
-        neg_mean_a = held.tile([D, 1], F32, name="neg_mean_a")
-        neg_mean_b = held.tile([D, 1], F32, name="neg_mean_b")
-        nc.vector.tensor_scalar(scaled[:, :HH], w_rows[:, :HH], -1.0 / H, None, ALU.mult, ALU.add, accum_out=neg_mean_a[:])
-        nc.scalar.activation(scaled[:, HH:], w_rows[:, HH:], ACT.Copy, scale=-1.0 / H, accum_out=neg_mean_b[:])
+        scaled = held.tile([D, H], BF16, name="scaled")
+        neg_mean = held.tile([D, 1], F32, name="neg_mean")
+        nc.vector.tensor_scalar(scaled[:], w_rows[:], -1.0 / H, None, ALU.mult, ALU.add, accum_out=neg_mean[:])
         w_by_block = w_rows[:].rearrange("k (p b) -> k b p", b=HB)
         w_hi = held.tile([D, HB, P], BF16, name="w_hi")
         w_lo = held.tile([D, HB, P], BF16, name="w_lo")
-        neg_mean = held.tile([D, 1], F32, name="neg_mean")
         for b in range(HB):
-            nc.vector.tensor_scalar(w_hi[:, b, :], w_by_block[:, b, :], neg_mean_a[:], neg_mean_b[:], ALU.add, ALU.add)
-            if b == 0:
-                nc.vector.tensor_tensor(neg_mean[:], neg_mean_a[:], neg_mean_b[:], ALU.add)
+            nc.vector.tensor_scalar(w_hi[:, b, :], w_by_block[:, b, :], neg_mean[:], None, ALU.add)
             nc.vector.scalar_tensor_tensor(
                 w_lo[:, b, :], w_by_block[:, b, :], neg_mean[:], w_hi[:, b, :], ALU.add, ALU.subtract
             )

@@ -77,9 +77,8 @@ def tile_lineattention_kernel(tc, table, w, gain, bias, offs, out):
         sum_b = held.tile([P, NW], F32, name="sum_b")
         nc.vector.tensor_tensor(sum_a[:], squares[:, 0, first], squares[:, 1, first], ALU.add)
         nc.vector.tensor_tensor(sum_b[:], sum_a[:], squares[:, 2, first], ALU.add)
-        nc.vector.tensor_tensor(sum_a[:], sum_b[:], squares[:, 3, first], ALU.add)
-        nc.vector.tensor_tensor(sum_b[:], squares[:, 0, second], squares[:, 1, second], ALU.add)
-        terms = [[sum_a[:]], [sum_b[:], squares[:, 2, second], squares[:, 3, second]]]
+        nc.vector.tensor_tensor(sum_a[:], squares[:, 0, second], squares[:, 1, second], ALU.add)
+        terms = [[sum_b[:], squares[:, HB - 1, first]], [sum_a[:], squares[:, 2, second], squares[:, 3, second]]]
         rstd = held.tile([P, N], F32, name="rstd")
         for h in range(NH):
             cols = slice(h * NW, (h + 1) * NW)

import concourse.mybir as mybir
from concourse.masks import make_identity

P = 128
S, D, H, N = 512, 128, 512, 256
SB = S // P
HB = H // P
NH = 2
NW = N // NH
EPS = 1e-5
FLOPS = 2 * D * H * N

BF16, F32, U16 = mybir.dt.bfloat16, mybir.dt.float32, mybir.dt.uint16
ACT = mybir.ActivationFunctionType
ALU = mybir.AluOpType
AXIS = mybir.AxisListType


def tile_lineattention_kernel(tc, table, w, gain, bias, offs, out):
    nc = tc.nc
    with tc.tile_pool(name="held", bufs=1) as held, tc.psum_pool(name="psum", bufs=1) as psum:
        table_rows = held.tile([P, SB, D], BF16, name="table_rows")
        table_blocks = table.rearrange("(s p) k -> p s k", p=P)
        w_rows = held.tile([D, H], BF16, name="w_rows")
        nc.sync.dma_start(table_rows[:, 0, :], table_blocks[:, 0, :])
        nc.sync.dma_start(w_rows[:], w)
        for s in range(1, SB):
            nc.sync.dma_start(table_rows[:, s, :], table_blocks[:, s, :])
        offsets = held.tile([P, N // 16], U16, name="offsets")
        nc.sync.dma_start(offsets[:], offs)
        gain_cols = held.tile([P, HB], F32, name="gain_cols")
        nc.sync.dma_start(gain_cols[:], gain.rearrange("(p b) one -> p (b one)", b=HB))
        bias_cols = held.tile([P, HB], F32, name="bias_cols")
        nc.sync.dma_start(bias_cols[:], bias.rearrange("(p b) one -> p (b one)", b=HB))
        out_blocks = out.rearrange("(p b) j -> p b j", b=HB)

        identity = held.tile([P, P], BF16, name="identity")
        make_identity(nc, identity[:])
        averaging = held.tile([P, P], F32, name="averaging")
        nc.vector.memset(averaging[:], 1.0 / H)
        eps_col = held.tile([P, 1], F32, name="eps_col")
        nc.vector.memset(eps_col[:], EPS)
        table_fetch = held.tile([P, 1], F32, name="table_fetch")
        nc.scalar.activation(table_fetch[:], eps_col[:], ACT.Abs_reciprocal_sqrt)

        table_cols = held.tile([D, S], BF16, name="table_cols")
        for s in range(SB):
            flipped_ps = psum.tile([D, P], BF16, name=f"flipped_ps{s}", tag=f"bank{s}")
            nc.tensor.transpose(flipped_ps[:], table_rows[:, s, :], identity[:])
            nc.scalar.copy(table_cols[:, s * P : (s + 1) * P], flipped_ps[:])

        scaled = held.tile([D, H], BF16, name="scaled")
        neg_mean = held.tile([D, 1], F32, name="neg_mean")
        nc.vector.tensor_scalar(scaled[:], w_rows[:], -1.0 / H, None, ALU.mult, ALU.add, accum_out=neg_mean[:])
        w_by_block = w_rows[:].rearrange("k (p b) -> k b p", b=HB)
        w_hi = held.tile([D, HB, P], BF16, name="w_hi")
        w_lo = held.tile([D, HB, P], BF16, name="w_lo")
        for b in range(HB):
            nc.vector.tensor_scalar(w_hi[:, b, :], w_by_block[:, b, :], neg_mean[:], None, ALU.add)
            nc.vector.scalar_tensor_tensor(
                w_lo[:, b, :], w_by_block[:, b, :], neg_mean[:], w_hi[:, b, :], ALU.add, ALU.subtract
            )

        centred_ps = [psum.tile([P, N], F32, name=f"centred_ps{b}", tag=f"bank{b}") for b in range(HB)]
        squares = held.tile([P, HB, N], F32, name="squares")
        for h in range(NH):
            cols = slice(h * NW, (h + 1) * NW)
            piece = offsets[:, h * (NW // 16) : (h + 1) * (NW // 16)]
            for b in range(HB):
                nc.tensor.matmul(centred_ps[b][:, cols], w_hi[:, b, :], table_cols[:].indirect(piece), start=True, stop=False)
                nc.tensor.matmul(centred_ps[b][:, cols], w_lo[:, b, :], table_cols[:].indirect(piece), start=False, stop=True)
                nc.scalar.activation(squares[:, b, cols], centred_ps[b][:, cols], ACT.Square)

        first = slice(0, NW)
        second = slice(NW, N)
        sum_a = held.tile([P, NW], F32, name="sum_a")
        sum_b = held.tile([P, NW], F32, name="sum_b")
        nc.vector.tensor_tensor(sum_a[:], squares[:, 0, first], squares[:, 1, first], ALU.add)
        nc.vector.tensor_tensor(sum_b[:], sum_a[:], squares[:, 2, first], ALU.add)
        nc.vector.tensor_tensor(sum_a[:], squares[:, 0, second], squares[:, 1, second], ALU.add)
        terms = [[sum_b[:], squares[:, HB - 1, first]], [sum_a[:], squares[:, 2, second], squares[:, 3, second]]]
        rstd = held.tile([P, N], F32, name="rstd")
        for h in range(NH):
            cols = slice(h * NW, (h + 1) * NW)
            var_ps = psum.tile([P, NW], F32, name=f"var_ps{h}")
            for i, term in enumerate(terms[h]):
                nc.tensor.matmul(var_ps[:], averaging[:], term, start=(i == 0), stop=(i == len(terms[h]) - 1))
            nc.scalar.activation(rstd[:, cols], var_ps[:], ACT.Abs_reciprocal_sqrt, bias=eps_col[:], scale=1.0)

        normed = held.tile([P, HB, N], F32, name="normed")
        result = held.tile([P, HB, N], F32, name="result")
        for h in range(NH):
            cols = slice(h * NW, (h + 1) * NW)
            for b in range(HB):
                nc.vector.tensor_tensor(normed[:, b, cols], centred_ps[b][:, cols], rstd[:, cols], ALU.mult)
                nc.vector.tensor_scalar(
                    result[:, b, cols], normed[:, b, cols], gain_cols[:, b : b + 1], bias_cols[:, b : b + 1], ALU.mult, ALU.add
                )
                nc.sync.dma_start(out_blocks[:, b, cols], result[:, b, cols])
